import numpy as np
import ml_dtypes


def mxq(x, axis, fmt="e4m3"):
    dtype, down = {"e4m3": (ml_dtypes.float8_e4m3fn, 7), "e5m2": (ml_dtypes.float8_e5m2, 14)}[fmt]
    v = np.moveaxis(np.asarray(x, np.float32).astype(ml_dtypes.bfloat16).astype(np.float64), axis, -1)
    blocks = v.reshape(v.shape[:-1] + (-1, 32))
    amax = np.abs(blocks).max(-1, keepdims=True)
    byte = np.maximum(np.where(amax > 0, np.frexp(amax)[1] - 1 + 127, 0) - down, 1)
    scale = np.exp2(byte - 127.0)
    codes = (blocks / scale).astype(np.float32).astype(dtype).astype(np.float64)
    return np.moveaxis((codes * scale).reshape(v.shape), -1, axis)


WIDE = False


def mx_kscale(k):
    if not WIDE:
        return np.ones(k)
    levels = np.array([10, -10, 5, -5, 0])
    a = np.random.permutation(np.resize(levels, k // 512 * 4)).reshape(k // 512, 4)
    idx = np.arange(k)
    return np.exp2(a[idx // 512, idx % 128 // 32])


BF16 = ml_dtypes.bfloat16


def bf(x):
    return np.asarray(x, np.float32).astype(BF16)


def f64(x):
    return np.asarray(x).astype(np.float64)


B, S_IMG, S_TXT, D, H, HD = 1, 768, 256, 1536, 12, 128
S = S_TXT + S_IMG
E = H * HD
EPS = 1e-5


def rmsnorm(x, w):
    var = np.mean(np.square(x), axis=-1, keepdims=True)
    return x * (1.0 / np.sqrt(var + EPS)) * w


def rope(x, cos, sin):
    xr = x.reshape(x.shape[:-1] + (HD // 2, 2))
    x_rot = np.stack([-xr[..., 1], xr[..., 0]], axis=-1).reshape(x.shape)
    return x * cos[None, :, None, :] + x_rot * sin[None, :, None, :]


def setup_inputs():
    r = np.random.standard_normal
    s, u = mx_kscale(D), mx_kscale(D)
    pw = 0.015 / np.sqrt(D)
    return {"hidden_states": bf(r((B, S_IMG, D)) * s),
            "encoder_hidden_states": bf(r((B, S_TXT, D)) * u),
            "rope_cos": bf(np.random.uniform(size=(S, HD))),
            "rope_sin": bf(np.random.uniform(size=(S, HD))),
            "Wq": bf(r((E, D)) * pw / s),
            "Wk": bf(r((E, D)) * pw / s),
            "Waq": bf(r((E, D)) * pw / u),
            "baq": bf(r(E) * 0.005),
            "Wak": bf(r((E, D)) * pw / u),
            "bak": bf(r(E) * 0.005),
            "wq_norm": bf(1.75 + 0.15 * r(HD)),
            "wk_norm": bf(1.75 + 0.15 * r(HD)),
            "waq_norm": bf(1.75 + 0.15 * r(HD)),
            "wak_norm": bf(1.75 + 0.15 * r(HD))}


def reference(hidden_states, encoder_hidden_states, rope_cos, rope_sin, Wq, Wk, Waq, baq, Wak, bak, wq_norm, wk_norm, waq_norm, wak_norm):
    xq = mxq(f64(hidden_states), 2, "e4m3")
    cq = mxq(f64(encoder_hidden_states), 2, "e4m3")
    q = (xq @ mxq(f64(Wq).T, 0, "e4m3")).reshape(B, S_IMG, H, HD)
    k = (xq @ mxq(f64(Wk).T, 0, "e4m3")).reshape(B, S_IMG, H, HD)
    q = rmsnorm(q, f64(wq_norm))
    k = rmsnorm(k, f64(wk_norm))
    eq = ((cq @ mxq(f64(Waq).T, 0, "e4m3")) + f64(baq)).reshape(B, S_TXT, H, HD)
    ek = ((cq @ mxq(f64(Wak).T, 0, "e4m3")) + f64(bak)).reshape(B, S_TXT, H, HD)
    eq = rmsnorm(eq, f64(waq_norm))
    ek = rmsnorm(ek, f64(wak_norm))
    q = np.concatenate([eq, q], axis=1)
    k = np.concatenate([ek, k], axis=1)
    return rope(q, f64(rope_cos), f64(rope_sin)), rope(k, f64(rope_cos), f64(rope_sin))

@@ -1,0 +1,296 @@
+from contextlib import ExitStack
+
+import concourse.mybir as mybir
+from concourse.masks import make_identity
+
+F32 = mybir.dt.float32
+BF16 = mybir.dt.bfloat16
+I32 = mybir.dt.int32
+U32 = mybir.dt.uint32
+U8 = mybir.dt.uint8
+FP8X4 = mybir.dt.float8_e4m3fn_x4
+ACT = mybir.ActivationFunctionType
+ALU = mybir.AluOpType
+
+P = 128
+D_MODEL = 1536
+WORDS = D_MODEL // 2
+K_PASS = 512
+PASSES = D_MODEL // K_PASS
+HEAD_DIM = 128
+PAIRS = HEAD_DIM // 2
+E_OUT = 1536
+CHUNK = 512
+CHUNK_HEADS = CHUNK // HEAD_DIM
+CHUNK_ROW_TILES = CHUNK // P
+CHUNKS = E_OUT // CHUNK
+TILES = 8
+DUO = 2
+DUOS = TILES // DUO
+TEXT_CHUNKS = 2 * CHUNKS
+EPS = 1e-5
+LOADS_AHEAD = 3
+STEPS_AHEAD = PASSES + 1
+
+FLOPS = 2 * 2 * 1024 * D_MODEL * E_OUT
+
+
+def tile_flux2attention_pa_kernel(
+    tc,
+    hidden_states,
+    encoder_hidden_states,
+    rope_cos,
+    rope_sin,
+    Wq,
+    Wk,
+    Waq,
+    baq,
+    Wak,
+    bak,
+    wq_norm,
+    wk_norm,
+    waq_norm,
+    wak_norm,
+    out_0,
+    out_1,
+):
+    nc = tc.nc
+    with ExitStack() as ctx:
+        ctx.enter_context(tc.manual_schedule())
+        const = ctx.enter_context(tc.tile_pool(name="const", bufs=1))
+        raw_pool = ctx.enter_context(tc.tile_pool(name="raw", bufs=LOADS_AHEAD + 1))
+        grouped_pool = ctx.enter_context(tc.tile_pool(name="grouped", bufs=4))
+        quant_pool = ctx.enter_context(tc.tile_pool(name="quant", bufs=3))
+        duo_pool = ctx.enter_context(tc.tile_pool(name="duo", bufs=2))
+        terms_pool = ctx.enter_context(tc.tile_pool(name="terms", bufs=6))
+        rotated_pool = ctx.enter_context(tc.tile_pool(name="rotated", bufs=8))
+        small = ctx.enter_context(tc.tile_pool(name="small", bufs=4))
+        psum_t = ctx.enter_context(tc.psum_pool(name="psum_t", bufs=4))
+        psum_acc = ctx.enter_context(tc.psum_pool(name="psum_acc", bufs=4))
+
+        x_txt = encoder_hidden_states[0].rearrange("(t p) k -> p t k", p=P)
+        x_img = hidden_states[0].rearrange("(t p) k -> p t k", p=P)
+        out_q = out_0[0].rearrange("(t p) h d -> p t (h d)", p=P)
+        out_k = out_1[0].rearrange("(t p) h d -> p t (h d)", p=P)
+
+        x_raw = const.tile([P, TILES, D_MODEL], BF16)
+        x_codes = const.tile([P, PASSES, TILES * P], U32, align_bytes=64)
+        x_scales = const.tile([P, PASSES, TILES * P], U8, align_bytes=64)
+        cos_sb = const.tile([P, TILES, PAIRS, 2], BF16)
+        sin_sb = const.tile([P, TILES, PAIRS, 2], BF16)
+        gain_rows = const.tile([P, 4 * HEAD_DIM], BF16)
+        bias_rows = const.tile([P, 2 * E_OUT], BF16)
+        gain_sb = const.tile([P, 4, HEAD_DIM], BF16)
+        bias_sb = const.tile([P, 2 * E_OUT], BF16)
+        one = const.tile([P, 1], F32)
+        unused = const.tile([P, 1], F32)
+        ones = const.tile([P, P], BF16)
+        ident = const.tile([P, P], F32)
+        rot = const.tile([P, TILES, 2, PAIRS, 2], F32)
+        factors_q = const.tile([P, TILES, 2, HEAD_DIM], F32)
+        factors_k = const.tile([P, TILES, 2, HEAD_DIM], F32)
+
+        jobs = (
+            (Waq, factors_q, out_q, (0,)),
+            (Wak, factors_k, out_k, (0,)),
+            (Wq, factors_q, out_q, (1, 2, 3)),
+            (Wk, factors_k, out_k, (1, 2, 3)),
+        )
+        chunks = [(job, c) for job in jobs for c in range(CHUNKS)]
+
+        def load_tokens(duo):
+            source = x_txt if duo == 0 else x_img[:, DUO * (duo - 1) : DUO * duo, :]
+            nc.sync.dma_start(out=x_raw[:, DUO * duo : DUO * (duo + 1), :], in_=source)
+
+        w_raw = {}
+
+        def load_chunk(n, pieces=1):
+            job, c = chunks[n]
+            w_raw[n] = raw_pool.tile([P, CHUNK_ROW_TILES, D_MODEL], BF16, name="w_raw")
+            rows = job[0][c * CHUNK : (c + 1) * CHUNK, :].rearrange("(r p) k -> p r k", p=P)
+            for i in range(pieces):
+                k_range = slice(i * D_MODEL // pieces, (i + 1) * D_MODEL // pieces)
+                nc.sync.dma_start(out=w_raw[n][:, :, k_range], in_=rows[:, :, k_range])
+
+        nc.vector.memset(gain_rows[:].bitcast(I32), 0)
+        nc.vector.memset(bias_rows[:].bitcast(I32), 0)
+        nc.vector.memset(ones[:], 1.0)
+        nc.vector.memset(one[:], 1.0)
+        make_identity(nc, ident[:])
+
+        for i, gain in enumerate((waq_norm, wak_norm, wq_norm, wk_norm)):
+            nc.scalar.dma_start(
+                out=gain_rows[0:1, i * HEAD_DIM : (i + 1) * HEAD_DIM], in_=gain.rearrange("(o d) -> o d", o=1)
+            )
+        for table_sb, table in ((cos_sb, rope_cos), (sin_sb, rope_sin)):
+            nc.scalar.dma_start(
+                out=table_sb[:].rearrange("p t i j -> p t (i j)"), in_=table.rearrange("(t p) d -> p t d", p=P)
+            )
+        nc.scalar.activation(out=unused[:], in_=one[:], func=ACT.Abs_reciprocal_sqrt)
+        for i, bias in enumerate((baq, bak)):
+            nc.gpsimd.dma_start(
+                out=bias_rows[0:1, i * E_OUT : (i + 1) * E_OUT], in_=bias.rearrange("(o e) -> o e", o=1)
+            )
+        load_tokens(0)
+        load_chunk(0, pieces=PASSES)
+        load_chunk(1)
+        load_tokens(1)
+        load_chunk(2)
+
+        def spread(rows, target):
+            bank = psum_acc.tile([P, CHUNK], F32, name="acc")
+            nc.tensor.matmul(out=bank[:], lhsT=ones[:], rhs=rows, start=True, stop=True)
+            nc.vector.tensor_copy(out=target, in_=bank[:])
+
+        def build_factors(duo):
+            tiles = slice(DUO * duo, DUO * (duo + 1))
+            for o, j, table, sign in ((0, 0, cos_sb, 1.0), (0, 1, sin_sb, -1.0), (1, 0, sin_sb, 1.0), (1, 1, cos_sb, 1.0)):
+                nc.gpsimd.tensor_scalar(
+                    out=rot[:, tiles, o, :, j], in0=table[:, tiles, :, o], scalar1=sign, scalar2=0.0, op0=ALU.mult, op1=ALU.add
+                )
+            stream = 0 if duo == 0 else 1
+            for i, factors in enumerate((factors_q, factors_k)):
+                nc.gpsimd.tensor_tensor(
+                    out=factors[:, tiles].rearrange("p t o d -> p (t o) d"),
+                    in0=rot[:, tiles].rearrange("p t o i j -> p (t o) (i j)"),
+                    in1=gain_sb[:, 2 * stream + i : 2 * stream + i + 1, :].to_broadcast([P, DUO * 2, HEAD_DIM]),
+                    op=ALU.mult,
+                )
+
+        def transpose_pass(rows_words, first_word, g, codes, scales, vector_helps):
+            n_cols = P * len(first_word)
+            grouped = grouped_pool.tile([P, 4 * CHUNK], BF16, align_bytes=64, name="grouped")
+            grouped_words = grouped[:].bitcast(F32).rearrange("p (c u) -> p c u", u=2)
+            for half in range(len(first_word) // 2):
+                xt = psum_t.tile([P, 2, 2 * P], F32, name="xt")
+                for u in range(2):
+                    for r in range(2):
+                        word = first_word[2 * half + r] + (K_PASS // 2) * g + P * u
+                        nc.tensor.transpose(xt[:, u, r * P : (r + 1) * P], rows_words[:, word : word + P], ident[:])
+                target = grouped_words[:, 2 * half * P : (2 * half + 2) * P, :]
+                if vector_helps and (g + half) % 2 == 1:
+                    nc.vector.tensor_copy(out=target, in_=xt[:].rearrange("p u c -> p c u"))
+                else:
+                    nc.scalar.copy(out=target, in_=xt[:].rearrange("p u c -> p c u"))
+            return (grouped[:, 0 : 4 * n_cols], codes, scales)
+
+        def quantise(grouped, codes, scales):
+            nc.vector.quantize_mx(out=codes.bitcast(FP8X4), scales=scales, in_=grouped)
+
+        def transpose_x(duo, g, vector_helps=False):
+            cols = slice(DUO * duo * P, DUO * (duo + 1) * P)
+            first_word = [t * WORDS for t in range(DUO * duo, DUO * (duo + 1))]
+            x_words = x_raw[:].rearrange("p t k -> p (t k)").bitcast(F32)
+            return transpose_pass(x_words, first_word, g, x_codes[:, g, cols], x_scales[:, g, cols], vector_helps)
+
+        w_codes = {}
+        w_scales = {}
+
+        def transpose_w(n, g, vector_helps=False):
+            if g == 0:
+                w_codes[n] = quant_pool.tile([P, PASSES, CHUNK], U32, align_bytes=64, name="w_codes")
+                w_scales[n] = quant_pool.tile([P, PASSES, CHUNK], U8, align_bytes=64, name="w_scales")
+            w_words = w_raw[n][:].rearrange("p r k -> p (r k)").bitcast(F32)
+            first_word = [r * WORDS for r in range(CHUNK_ROW_TILES)]
+            return transpose_pass(w_words, first_word, g, w_codes[n][:, g, :], w_scales[n][:, g, :], vector_helps)
+
+        def project(n, duo):
+            xs = []
+            for t in range(DUO * duo, DUO * (duo + 1)):
+                acc = psum_acc.tile([P, CHUNK], F32, name="acc")
+                for g in range(PASSES):
+                    nc.tensor.matmul_mx(
+                        out=acc[:],
+                        lhsT=x_codes[:, g, t * P : (t + 1) * P].bitcast(FP8X4),
+                        lhsT_scale=x_scales[:, g, t * P : (t + 1) * P],
+                        rhs=w_codes[n][:, g, :].bitcast(FP8X4),
+                        rhs_scale=w_scales[n][:, g, :],
+                        start=(g == 0),
+                        stop=(g == PASSES - 1),
+                    )
+                xs.append(acc)
+            if n < TEXT_CHUNKS:
+                biased = duo_pool.tile([P, DUO, CHUNK], F32, name="biased")
+                for i in range(DUO):
+                    nc.vector.tensor_tensor(
+                        out=biased[:, i, :], in0=xs[i][:], in1=bias_sb[:, n * CHUNK : (n + 1) * CHUNK], op=ALU.add
+                    )
+                xs = [biased[:, i, :] for i in range(DUO)]
+            else:
+                xs = [acc[:] for acc in xs]
+
+            squares = duo_pool.tile([P, DUO, CHUNK], F32, name="squares")
+            sum_sq = small.tile([P, DUO * CHUNK_HEADS], F32, name="sum_sq")
+            for i in range(DUO):
+                for h in range(CHUNK_HEADS):
+                    head = slice(h * HEAD_DIM, (h + 1) * HEAD_DIM)
+                    k = i * CHUNK_HEADS + h
+                    nc.scalar.activation(
+                        out=squares[:, i, head], in_=xs[i][:, head], func=ACT.Square, accum_out=sum_sq[:, k : k + 1]
+                    )
+            r = small.tile([P, DUO * CHUNK_HEADS], F32, name="r")
+            nc.scalar.activation(out=r[:], in_=sum_sq[:], func=ACT.Abs_reciprocal_sqrt, scale=1.0 / HEAD_DIM, bias=EPS)
+            return (n, duo, xs, r)
+
+        def rotate(n, duo, xs, r):
+            job, c = chunks[n]
+            factors, out_rows = job[1], job[2]
+            for i in range(DUO):
+                t = DUO * duo + i
+                terms = terms_pool.tile([P, CHUNK_HEADS, 2, PAIRS, 2], F32, name="terms")
+                for h in range(CHUNK_HEADS):
+                    k = i * CHUNK_HEADS + h
+                    nc.vector.scalar_tensor_tensor(
+                        out=terms[:, h].rearrange("p o i j -> p o (i j)"),
+                        in0=xs[i][:, h * HEAD_DIM : (h + 1) * HEAD_DIM].unsqueeze(1).to_broadcast([P, 2, HEAD_DIM]),
+                        scalar=r[:, k : k + 1],
+                        in1=factors[:, t],
+                        op0=ALU.mult,
+                        op1=ALU.mult,
+                    )
+                rotated = rotated_pool.tile([P, CHUNK_HEADS, PAIRS, 2], F32, name="rotated")
+                by_output = terms[:].rearrange("p h o i j -> p h i o j")
+                nc.gpsimd.tensor_tensor(
+                    out=rotated[:], in0=by_output[:, :, :, :, 0], in1=by_output[:, :, :, :, 1], op=ALU.add
+                )
+                nc.sync.dma_start(
+                    out=out_rows[:, t, c * CHUNK : (c + 1) * CHUNK], in_=rotated[:].rearrange("p h i o -> p (h i o)")
+                )
+
+        def spread_bias(n):
+            spread(bias_rows[:, n * CHUNK : (n + 1) * CHUNK], bias_sb[:, n * CHUNK : (n + 1) * CHUNK])
+
+        for g in range(PASSES):
+            quantise(*transpose_x(0, g, vector_helps=True))
+        spread(gain_rows[:], gain_sb[:].rearrange("p i d -> p (i d)"))
+        build_factors(0)
+        spread_bias(0)
+        units = [(n, g) for n in range(len(chunks)) for g in range(PASSES)]
+        for n, g in units[0:STEPS_AHEAD]:
+            quantise(*transpose_w(n, g, vector_helps=True))
+
+        multiplied = None
+        for n in range(len(chunks)):
+            if n + LOADS_AHEAD < len(chunks):
+                load_chunk(n + LOADS_AHEAD)
+            if n + 2 < DUOS:
+                load_tokens(n + 2)
+            if n + 1 < DUOS:
+                build_factors(n + 1)
+            if n + 1 < TEXT_CHUNKS:
+                spread_bias(n + 1)
+            duos = chunks[n][0][3]
+            for g in range(PASSES):
+                copied = []
+                ahead = n * PASSES + g + STEPS_AHEAD
+                if ahead < len(units):
+                    copied.append(transpose_w(*units[ahead]))
+                if n + 1 < DUOS:
+                    copied.append(transpose_x(n + 1, g))
+                before = multiplied
+                multiplied = project(n, duos[g]) if g < len(duos) else None
+                if before is not None:
+                    rotate(*before)
+                for piece in copied:
+                    quantise(*piece)
+        rotate(*multiplied)

@@ -25,12 +25,13 @@ CHUNK_HEADS = CHUNK // HEAD_DIM
 CHUNK_ROW_TILES = CHUNK // P
 CHUNKS = E_OUT // CHUNK
 TILES = 8
+TEXT_TILES = 2
 DUO = 2
-DUOS = TILES // DUO
-TEXT_CHUNKS = 2 * CHUNKS
+TEXT_DUOS = (0,)
+IMAGE_DUOS = (1, 2, 3)
 EPS = 1e-5
-LOADS_AHEAD = 3
-STEPS_AHEAD = PASSES + 1
+RAW_CHUNKS = 4
+LEAD = 3
 
 FLOPS = 2 * 2 * 1024 * D_MODEL * E_OUT
 
@@ -58,12 +59,13 @@ def tile_flux2attention_pa_kernel(
     with ExitStack() as ctx:
         ctx.enter_context(tc.manual_schedule())
         const = ctx.enter_context(tc.tile_pool(name="const", bufs=1))
-        raw_pool = ctx.enter_context(tc.tile_pool(name="raw", bufs=LOADS_AHEAD + 1))
-        grouped_pool = ctx.enter_context(tc.tile_pool(name="grouped", bufs=4))
+        raw_pool = ctx.enter_context(tc.tile_pool(name="raw", bufs=RAW_CHUNKS))
+        grouped_w_pool = ctx.enter_context(tc.tile_pool(name="grouped_w", bufs=5))
+        grouped_x_pool = ctx.enter_context(tc.tile_pool(name="grouped_x", bufs=4))
         quant_pool = ctx.enter_context(tc.tile_pool(name="quant", bufs=3))
         duo_pool = ctx.enter_context(tc.tile_pool(name="duo", bufs=2))
-        terms_pool = ctx.enter_context(tc.tile_pool(name="terms", bufs=6))
-        rotated_pool = ctx.enter_context(tc.tile_pool(name="rotated", bufs=8))
+        terms_pool = ctx.enter_context(tc.tile_pool(name="terms", bufs=5))
+        rotated_pool = ctx.enter_context(tc.tile_pool(name="rotated", bufs=6))
         small = ctx.enter_context(tc.tile_pool(name="small", bufs=4))
         psum_t = ctx.enter_context(tc.psum_pool(name="psum_t", bufs=4))
         psum_acc = ctx.enter_context(tc.psum_pool(name="psum_acc", bufs=4))
@@ -90,24 +92,28 @@ def tile_flux2attention_pa_kernel(
         factors_q = const.tile([P, TILES, 2, HEAD_DIM], F32)
         factors_k = const.tile([P, TILES, 2, HEAD_DIM], F32)
 
-        jobs = (
-            (Waq, factors_q, out_q, (0,)),
-            (Wak, factors_k, out_k, (0,)),
-            (Wq, factors_q, out_q, (1, 2, 3)),
-            (Wk, factors_k, out_k, (1, 2, 3)),
-        )
-        chunks = [(job, c) for job in jobs for c in range(CHUNKS)]
+        chunks = []
+        for w_img, w_txt, bias_col, factors, out_rows in (
+            (Wq, Waq, 0, factors_q, out_q),
+            (Wk, Wak, E_OUT, factors_k, out_k),
+        ):
+            for c in range(CHUNKS):
+                chunks.append((w_img, c * CHUNK, None, factors, out_rows, IMAGE_DUOS))
+                chunks.append((w_txt, c * CHUNK, bias_col + c * CHUNK, factors, out_rows, TEXT_DUOS))
+        works = [(n, duo) for n in range(len(chunks)) for duo in chunks[n][5]]
+        units = [(n, g) for n in range(len(chunks)) for g in range(PASSES)]
+        first_duos = [duo for n, duo in works[0 : len(TEXT_DUOS) + len(IMAGE_DUOS)]]
 
         def load_tokens(duo):
-            source = x_txt if duo == 0 else x_img[:, DUO * (duo - 1) : DUO * duo, :]
+            source = x_txt if duo in TEXT_DUOS else x_img[:, DUO * duo - TEXT_TILES : DUO * (duo + 1) - TEXT_TILES, :]
             nc.sync.dma_start(out=x_raw[:, DUO * duo : DUO * (duo + 1), :], in_=source)
 
         w_raw = {}
 
         def load_chunk(n, pieces=1):
-            job, c = chunks[n]
+            weight, e0 = chunks[n][0], chunks[n][1]
             w_raw[n] = raw_pool.tile([P, CHUNK_ROW_TILES, D_MODEL], BF16, name="w_raw")
-            rows = job[0][c * CHUNK : (c + 1) * CHUNK, :].rearrange("(r p) k -> p r k", p=P)
+            rows = weight[e0 : e0 + CHUNK, :].rearrange("(r p) k -> p r k", p=P)
             for i in range(pieces):
                 k_range = slice(i * D_MODEL // pieces, (i + 1) * D_MODEL // pieces)
                 nc.sync.dma_start(out=w_raw[n][:, :, k_range], in_=rows[:, :, k_range])
@@ -118,7 +124,7 @@ def tile_flux2attention_pa_kernel(
         nc.vector.memset(one[:], 1.0)
         make_identity(nc, ident[:])
 
-        for i, gain in enumerate((waq_norm, wak_norm, wq_norm, wk_norm)):
+        for i, gain in enumerate((wq_norm, wk_norm, waq_norm, wak_norm)):
             nc.scalar.dma_start(
                 out=gain_rows[0:1, i * HEAD_DIM : (i + 1) * HEAD_DIM], in_=gain.rearrange("(o d) -> o d", o=1)
             )
@@ -131,35 +137,25 @@ def tile_flux2attention_pa_kernel(
             nc.gpsimd.dma_start(
                 out=bias_rows[0:1, i * E_OUT : (i + 1) * E_OUT], in_=bias.rearrange("(o e) -> o e", o=1)
             )
-        load_tokens(0)
+        load_tokens(first_duos[0])
         load_chunk(0, pieces=PASSES)
+        load_tokens(first_duos[1])
+        load_tokens(first_duos[2])
         load_chunk(1)
-        load_tokens(1)
-        load_chunk(2)
+        load_tokens(first_duos[3])
+        for n in range(2, RAW_CHUNKS):
+            load_chunk(n)
 
         def spread(rows, target):
             bank = psum_acc.tile([P, CHUNK], F32, name="acc")
             nc.tensor.matmul(out=bank[:], lhsT=ones[:], rhs=rows, start=True, stop=True)
-            nc.vector.tensor_copy(out=target, in_=bank[:])
+            nc.scalar.copy(out=target, in_=bank[:])
 
-        def build_factors(duo):
-            tiles = slice(DUO * duo, DUO * (duo + 1))
-            for o, j, table, sign in ((0, 0, cos_sb, 1.0), (0, 1, sin_sb, -1.0), (1, 0, sin_sb, 1.0), (1, 1, cos_sb, 1.0)):
-                nc.gpsimd.tensor_scalar(
-                    out=rot[:, tiles, o, :, j], in0=table[:, tiles, :, o], scalar1=sign, scalar2=0.0, op0=ALU.mult, op1=ALU.add
-                )
-            stream = 0 if duo == 0 else 1
-            for i, factors in enumerate((factors_q, factors_k)):
-                nc.gpsimd.tensor_tensor(
-                    out=factors[:, tiles].rearrange("p t o d -> p (t o) d"),
-                    in0=rot[:, tiles].rearrange("p t o i j -> p (t o) (i j)"),
-                    in1=gain_sb[:, 2 * stream + i : 2 * stream + i + 1, :].to_broadcast([P, DUO * 2, HEAD_DIM]),
-                    op=ALU.mult,
-                )
+        def spread_bias(n):
+            cols = slice(chunks[n][2], chunks[n][2] + CHUNK)
+            spread(bias_rows[:, cols], bias_sb[:, cols])
 
-        def transpose_pass(rows_words, first_word, g, codes, scales, vector_helps):
-            n_cols = P * len(first_word)
-            grouped = grouped_pool.tile([P, 4 * CHUNK], BF16, align_bytes=64, name="grouped")
+        def transpose_pass(rows_words, first_word, g, grouped, codes, scales, vector_helps):
             grouped_words = grouped[:].bitcast(F32).rearrange("p (c u) -> p c u", u=2)
             for half in range(len(first_word) // 2):
                 xt = psum_t.tile([P, 2, 2 * P], F32, name="xt")
@@ -172,7 +168,7 @@ def tile_flux2attention_pa_kernel(
                     nc.vector.tensor_copy(out=target, in_=xt[:].rearrange("p u c -> p c u"))
                 else:
                     nc.scalar.copy(out=target, in_=xt[:].rearrange("p u c -> p c u"))
-            return (grouped[:, 0 : 4 * n_cols], codes, scales)
+            return (grouped[:], codes, scales)
 
         def quantise(grouped, codes, scales):
             nc.vector.quantize_mx(out=codes.bitcast(FP8X4), scales=scales, in_=grouped)
@@ -181,7 +177,8 @@ def tile_flux2attention_pa_kernel(
             cols = slice(DUO * duo * P, DUO * (duo + 1) * P)
             first_word = [t * WORDS for t in range(DUO * duo, DUO * (duo + 1))]
             x_words = x_raw[:].rearrange("p t k -> p (t k)").bitcast(F32)
-            return transpose_pass(x_words, first_word, g, x_codes[:, g, cols], x_scales[:, g, cols], vector_helps)
+            grouped = grouped_x_pool.tile([P, 4 * DUO * P], BF16, align_bytes=64, name="grouped_x")
+            return transpose_pass(x_words, first_word, g, grouped, x_codes[:, g, cols], x_scales[:, g, cols], vector_helps)
 
         w_codes = {}
         w_scales = {}
@@ -192,9 +189,11 @@ def tile_flux2attention_pa_kernel(
                 w_scales[n] = quant_pool.tile([P, PASSES, CHUNK], U8, align_bytes=64, name="w_scales")
             w_words = w_raw[n][:].rearrange("p r k -> p (r k)").bitcast(F32)
             first_word = [r * WORDS for r in range(CHUNK_ROW_TILES)]
-            return transpose_pass(w_words, first_word, g, w_codes[n][:, g, :], w_scales[n][:, g, :], vector_helps)
+            grouped = grouped_w_pool.tile([P, 4 * CHUNK], BF16, align_bytes=64, name="grouped_w")
+            return transpose_pass(w_words, first_word, g, grouped, w_codes[n][:, g, :], w_scales[n][:, g, :], vector_helps)
 
         def project(n, duo):
+            bias_col = chunks[n][2]
             xs = []
             for t in range(DUO * duo, DUO * (duo + 1)):
                 acc = psum_acc.tile([P, CHUNK], F32, name="acc")
@@ -208,18 +207,16 @@ def tile_flux2attention_pa_kernel(
                         start=(g == 0),
                         stop=(g == PASSES - 1),
                     )
-                xs.append(acc)
-            if n < TEXT_CHUNKS:
+                xs.append(acc[:])
+            if bias_col is not None:
                 biased = duo_pool.tile([P, DUO, CHUNK], F32, name="biased")
                 for i in range(DUO):
                     nc.vector.tensor_tensor(
-                        out=biased[:, i, :], in0=xs[i][:], in1=bias_sb[:, n * CHUNK : (n + 1) * CHUNK], op=ALU.add
+                        out=biased[:, i, :], in0=xs[i], in1=bias_sb[:, bias_col : bias_col + CHUNK], op=ALU.add
                     )
                 xs = [biased[:, i, :] for i in range(DUO)]
-            else:
-                xs = [acc[:] for acc in xs]
 
-            squares = duo_pool.tile([P, DUO, CHUNK], F32, name="squares")
+            squares = duo_pool.tile([P, DUO, CHUNK], BF16, name="squares")
             sum_sq = small.tile([P, DUO * CHUNK_HEADS], F32, name="sum_sq")
             for i in range(DUO):
                 for h in range(CHUNK_HEADS):
@@ -233,8 +230,7 @@ def tile_flux2attention_pa_kernel(
             return (n, duo, xs, r)
 
         def rotate(n, duo, xs, r):
-            job, c = chunks[n]
-            factors, out_rows = job[1], job[2]
+            e0, factors, out_rows = chunks[n][1], chunks[n][3], chunks[n][4]
             for i in range(DUO):
                 t = DUO * duo + i
                 terms = terms_pool.tile([P, CHUNK_HEADS, 2, PAIRS, 2], F32, name="terms")
@@ -253,44 +249,52 @@ def tile_flux2attention_pa_kernel(
                 nc.gpsimd.tensor_tensor(
                     out=rotated[:], in0=by_output[:, :, :, :, 0], in1=by_output[:, :, :, :, 1], op=ALU.add
                 )
-                nc.sync.dma_start(
-                    out=out_rows[:, t, c * CHUNK : (c + 1) * CHUNK], in_=rotated[:].rearrange("p h i o -> p (h i o)")
-                )
+                nc.sync.dma_start(out=out_rows[:, t, e0 : e0 + CHUNK], in_=rotated[:].rearrange("p h i o -> p (h i o)"))
 
-        def spread_bias(n):
-            spread(bias_rows[:, n * CHUNK : (n + 1) * CHUNK], bias_sb[:, n * CHUNK : (n + 1) * CHUNK])
+        nc.vector.tensor_copy(out=rot[:, :, 0, :, 0], in_=cos_sb[:, :, :, 0])
+        nc.vector.tensor_scalar_mul(out=rot[:, :, 0, :, 1], in0=sin_sb[:, :, :, 0], scalar1=-1.0)
+        nc.vector.tensor_copy(out=rot[:, :, 1, :, 0], in_=sin_sb[:, :, :, 1])
+        nc.vector.tensor_copy(out=rot[:, :, 1, :, 1], in_=cos_sb[:, :, :, 1])
+
+        def build_factors(factors, first_tile, n_tiles, gain_index):
+            tiles = slice(first_tile, first_tile + n_tiles)
+            nc.vector.tensor_tensor(
+                out=factors[:, tiles].rearrange("p t o d -> p (t o) d"),
+                in0=rot[:, tiles].rearrange("p t o i j -> p (t o) (i j)"),
+                in1=gain_sb[:, gain_index : gain_index + 1, :].to_broadcast([P, n_tiles * 2, HEAD_DIM]),
+                op=ALU.mult,
+            )
 
         for g in range(PASSES):
-            quantise(*transpose_x(0, g, vector_helps=True))
+            quantise(*transpose_x(first_duos[0], g, vector_helps=True))
         spread(gain_rows[:], gain_sb[:].rearrange("p i d -> p (i d)"))
-        build_factors(0)
-        spread_bias(0)
-        units = [(n, g) for n in range(len(chunks)) for g in range(PASSES)]
-        for n, g in units[0:STEPS_AHEAD]:
+        for n, g in units[0:PASSES]:
             quantise(*transpose_w(n, g, vector_helps=True))
+        for i, factors in enumerate((factors_q, factors_k)):
+            build_factors(factors, TEXT_TILES, TILES - TEXT_TILES, i)
+            build_factors(factors, 0, TEXT_TILES, 2 + i)
+        spread_bias(1)
 
+        prepared = PASSES
         multiplied = None
-        for n in range(len(chunks)):
-            if n + LOADS_AHEAD < len(chunks):
-                load_chunk(n + LOADS_AHEAD)
-            if n + 2 < DUOS:
-                load_tokens(n + 2)
-            if n + 1 < DUOS:
-                build_factors(n + 1)
-            if n + 1 < TEXT_CHUNKS:
-                spread_bias(n + 1)
-            duos = chunks[n][0][3]
-            for g in range(PASSES):
-                copied = []
-                ahead = n * PASSES + g + STEPS_AHEAD
-                if ahead < len(units):
-                    copied.append(transpose_w(*units[ahead]))
-                if n + 1 < DUOS:
-                    copied.append(transpose_x(n + 1, g))
-                before = multiplied
-                multiplied = project(n, duos[g]) if g < len(duos) else None
-                if before is not None:
-                    rotate(*before)
-                for piece in copied:
-                    quantise(*piece)
+        for step, (n, duo) in enumerate(works):
+            if step == 0 or works[step - 1][0] != n:
+                if n + RAW_CHUNKS < len(chunks):
+                    load_chunk(n + RAW_CHUNKS)
+                if chunks[n][2] is not None and n + 2 < len(chunks):
+                    spread_bias(n + 2)
+            copied = []
+            if step + 1 < len(first_duos):
+                for g in range(PASSES):
+                    copied.append(transpose_x(first_duos[step + 1], g))
+            wanted = min(len(units), PASSES * step, 3 * (step + 1 + LEAD) // 2)
+            for n_ahead, g in units[prepared:wanted]:
+                copied.append(transpose_w(n_ahead, g))
+            prepared = max(prepared, wanted)
+            before = multiplied
+            multiplied = project(n, duo)
+            if before is not None:
+                rotate(*before)
+            for piece in copied:
+                quantise(*piece)
         rotate(*multiplied)

@@ -26,12 +26,12 @@ CHUNK_ROW_TILES = CHUNK // P
 CHUNKS = E_OUT // CHUNK
 TILES = 8
 TEXT_TILES = 2
-DUO = 2
-TEXT_DUOS = (0,)
-IMAGE_DUOS = (1, 2, 3)
+UNIT_ROW_TILES = 2
+UNIT_ROWS = UNIT_ROW_TILES * P
 EPS = 1e-5
 RAW_CHUNKS = 4
-LEAD = 3
+UNITS_A_STEP_AT_FIRST = 3
+LEAD = 7
 
 FLOPS = 2 * 2 * 1024 * D_MODEL * E_OUT
 
@@ -60,13 +60,12 @@ def tile_flux2attention_pa_kernel(
         ctx.enter_context(tc.manual_schedule())
         const = ctx.enter_context(tc.tile_pool(name="const", bufs=1))
         raw_pool = ctx.enter_context(tc.tile_pool(name="raw", bufs=RAW_CHUNKS))
-        grouped_w_pool = ctx.enter_context(tc.tile_pool(name="grouped_w", bufs=5))
-        grouped_x_pool = ctx.enter_context(tc.tile_pool(name="grouped_x", bufs=4))
+        grouped_pool = ctx.enter_context(tc.tile_pool(name="grouped", bufs=8))
         quant_pool = ctx.enter_context(tc.tile_pool(name="quant", bufs=3))
-        duo_pool = ctx.enter_context(tc.tile_pool(name="duo", bufs=2))
+        work = ctx.enter_context(tc.tile_pool(name="work", bufs=3))
         terms_pool = ctx.enter_context(tc.tile_pool(name="terms", bufs=5))
         rotated_pool = ctx.enter_context(tc.tile_pool(name="rotated", bufs=6))
-        small = ctx.enter_context(tc.tile_pool(name="small", bufs=4))
+        small = ctx.enter_context(tc.tile_pool(name="small", bufs=6))
         psum_t = ctx.enter_context(tc.psum_pool(name="psum_t", bufs=4))
         psum_acc = ctx.enter_context(tc.psum_pool(name="psum_acc", bufs=4))
 
@@ -98,15 +97,27 @@ def tile_flux2attention_pa_kernel(
             (Wk, Wak, E_OUT, factors_k, out_k),
         ):
             for c in range(CHUNKS):
-                chunks.append((w_img, c * CHUNK, None, factors, out_rows, IMAGE_DUOS))
-                chunks.append((w_txt, c * CHUNK, bias_col + c * CHUNK, factors, out_rows, TEXT_DUOS))
-        works = [(n, duo) for n in range(len(chunks)) for duo in chunks[n][5]]
-        units = [(n, g) for n in range(len(chunks)) for g in range(PASSES)]
-        first_duos = [duo for n, duo in works[0 : len(TEXT_DUOS) + len(IMAGE_DUOS)]]
+                chunks.append((w_img, c * CHUNK, None, factors, out_rows, range(TEXT_TILES, TILES)))
+                chunks.append((w_txt, c * CHUNK, bias_col + c * CHUNK, factors, out_rows, range(TEXT_TILES)))
+        works = [(n, t) for n in range(len(chunks)) for t in chunks[n][5]]
 
-        def load_tokens(duo):
-            source = x_txt if duo in TEXT_DUOS else x_img[:, DUO * duo - TEXT_TILES : DUO * (duo + 1) - TEXT_TILES, :]
-            nc.sync.dma_start(out=x_raw[:, DUO * duo : DUO * (duo + 1), :], in_=source)
+        needs = []
+        for n, t in works:
+            for need in (("x", t // UNIT_ROW_TILES), ("w", n)):
+                if need not in needs:
+                    needs.append(need)
+        units = []
+        for kind, which in needs:
+            row_tiles = UNIT_ROW_TILES if kind == "x" else CHUNK_ROW_TILES
+            for g in range(PASSES):
+                for r in range(0, row_tiles, UNIT_ROW_TILES):
+                    units.append((kind, which, g, r))
+        units_before_the_loop = PASSES + PASSES * CHUNK_ROW_TILES // UNIT_ROW_TILES
+
+        def load_tokens(pair):
+            t0 = UNIT_ROW_TILES * pair
+            stream, first = (x_txt, t0) if t0 < TEXT_TILES else (x_img, t0 - TEXT_TILES)
+            nc.sync.dma_start(out=x_raw[:, t0 : t0 + UNIT_ROW_TILES, :], in_=stream[:, first : first + UNIT_ROW_TILES, :])
 
         w_raw = {}
 
@@ -137,14 +148,11 @@ def tile_flux2attention_pa_kernel(
             nc.gpsimd.dma_start(
                 out=bias_rows[0:1, i * E_OUT : (i + 1) * E_OUT], in_=bias.rearrange("(o e) -> o e", o=1)
             )
-        load_tokens(first_duos[0])
-        load_chunk(0, pieces=PASSES)
-        load_tokens(first_duos[1])
-        load_tokens(first_duos[2])
-        load_chunk(1)
-        load_tokens(first_duos[3])
-        for n in range(2, RAW_CHUNKS):
-            load_chunk(n)
+        for kind, which in needs:
+            if kind == "x":
+                load_tokens(which)
+            elif which < RAW_CHUNKS:
+                load_chunk(which, pieces=(PASSES if which == 0 else 1))
 
         def spread(rows, target):
             bank = psum_acc.tile([P, CHUNK], F32, name="acc")
@@ -155,101 +163,82 @@ def tile_flux2attention_pa_kernel(
             cols = slice(chunks[n][2], chunks[n][2] + CHUNK)
             spread(bias_rows[:, cols], bias_sb[:, cols])
 
-        def transpose_pass(rows_words, first_word, g, grouped, codes, scales, vector_helps):
+        w_codes = {}
+        w_scales = {}
+
+        def transpose_unit(kind, which, g, r0, vector_copies=False):
+            if kind == "x":
+                words = x_raw[:].rearrange("p t k -> p (t k)").bitcast(F32)
+                r0 = UNIT_ROW_TILES * which
+                codes, scales = x_codes, x_scales
+            else:
+                if g == 0 and r0 == 0:
+                    w_codes[which] = quant_pool.tile([P, PASSES, CHUNK], U32, align_bytes=64, name="w_codes")
+                    w_scales[which] = quant_pool.tile([P, PASSES, CHUNK], U8, align_bytes=64, name="w_scales")
+                words = w_raw[which][:].rearrange("p r k -> p (r k)").bitcast(F32)
+                codes, scales = w_codes[which], w_scales[which]
+            xt = psum_t.tile([P, 2, UNIT_ROWS], F32, name="xt")
+            for u in range(2):
+                for r in range(UNIT_ROW_TILES):
+                    word = (r0 + r) * WORDS + (K_PASS // 2) * g + P * u
+                    nc.tensor.transpose(xt[:, u, r * P : (r + 1) * P], words[:, word : word + P], ident[:])
+            grouped = grouped_pool.tile([P, 4 * UNIT_ROWS], BF16, align_bytes=64, name="grouped")
             grouped_words = grouped[:].bitcast(F32).rearrange("p (c u) -> p c u", u=2)
-            for half in range(len(first_word) // 2):
-                xt = psum_t.tile([P, 2, 2 * P], F32, name="xt")
-                for u in range(2):
-                    for r in range(2):
-                        word = first_word[2 * half + r] + (K_PASS // 2) * g + P * u
-                        nc.tensor.transpose(xt[:, u, r * P : (r + 1) * P], rows_words[:, word : word + P], ident[:])
-                target = grouped_words[:, 2 * half * P : (2 * half + 2) * P, :]
-                if vector_helps and (g + half) % 2 == 1:
-                    nc.vector.tensor_copy(out=target, in_=xt[:].rearrange("p u c -> p c u"))
-                else:
-                    nc.scalar.copy(out=target, in_=xt[:].rearrange("p u c -> p c u"))
-            return (grouped[:], codes, scales)
+            if vector_copies:
+                nc.vector.tensor_copy(out=grouped_words, in_=xt[:].rearrange("p u c -> p c u"))
+            else:
+                nc.scalar.copy(out=grouped_words, in_=xt[:].rearrange("p u c -> p c u"))
+            cols = slice(r0 * P, r0 * P + UNIT_ROWS)
+            return (grouped[:], codes[:, g, cols], scales[:, g, cols])
 
         def quantise(grouped, codes, scales):
             nc.vector.quantize_mx(out=codes.bitcast(FP8X4), scales=scales, in_=grouped)
 
-        def transpose_x(duo, g, vector_helps=False):
-            cols = slice(DUO * duo * P, DUO * (duo + 1) * P)
-            first_word = [t * WORDS for t in range(DUO * duo, DUO * (duo + 1))]
-            x_words = x_raw[:].rearrange("p t k -> p (t k)").bitcast(F32)
-            grouped = grouped_x_pool.tile([P, 4 * DUO * P], BF16, align_bytes=64, name="grouped_x")
-            return transpose_pass(x_words, first_word, g, grouped, x_codes[:, g, cols], x_scales[:, g, cols], vector_helps)
-
-        w_codes = {}
-        w_scales = {}
-
-        def transpose_w(n, g, vector_helps=False):
-            if g == 0:
-                w_codes[n] = quant_pool.tile([P, PASSES, CHUNK], U32, align_bytes=64, name="w_codes")
-                w_scales[n] = quant_pool.tile([P, PASSES, CHUNK], U8, align_bytes=64, name="w_scales")
-            w_words = w_raw[n][:].rearrange("p r k -> p (r k)").bitcast(F32)
-            first_word = [r * WORDS for r in range(CHUNK_ROW_TILES)]
-            grouped = grouped_w_pool.tile([P, 4 * CHUNK], BF16, align_bytes=64, name="grouped_w")
-            return transpose_pass(w_words, first_word, g, grouped, w_codes[n][:, g, :], w_scales[n][:, g, :], vector_helps)
-
-        def project(n, duo):
+        def project(n, t):
             bias_col = chunks[n][2]
-            xs = []
-            for t in range(DUO * duo, DUO * (duo + 1)):
-                acc = psum_acc.tile([P, CHUNK], F32, name="acc")
-                for g in range(PASSES):
-                    nc.tensor.matmul_mx(
-                        out=acc[:],
-                        lhsT=x_codes[:, g, t * P : (t + 1) * P].bitcast(FP8X4),
-                        lhsT_scale=x_scales[:, g, t * P : (t + 1) * P],
-                        rhs=w_codes[n][:, g, :].bitcast(FP8X4),
-                        rhs_scale=w_scales[n][:, g, :],
-                        start=(g == 0),
-                        stop=(g == PASSES - 1),
-                    )
-                xs.append(acc[:])
-            if bias_col is not None:
-                biased = duo_pool.tile([P, DUO, CHUNK], F32, name="biased")
-                for i in range(DUO):
-                    nc.vector.tensor_tensor(
-                        out=biased[:, i, :], in0=xs[i], in1=bias_sb[:, bias_col : bias_col + CHUNK], op=ALU.add
-                    )
-                xs = [biased[:, i, :] for i in range(DUO)]
-
-            squares = duo_pool.tile([P, DUO, CHUNK], BF16, name="squares")
-            sum_sq = small.tile([P, DUO * CHUNK_HEADS], F32, name="sum_sq")
-            for i in range(DUO):
-                for h in range(CHUNK_HEADS):
-                    head = slice(h * HEAD_DIM, (h + 1) * HEAD_DIM)
-                    k = i * CHUNK_HEADS + h
-                    nc.scalar.activation(
-                        out=squares[:, i, head], in_=xs[i][:, head], func=ACT.Square, accum_out=sum_sq[:, k : k + 1]
-                    )
-            r = small.tile([P, DUO * CHUNK_HEADS], F32, name="r")
-            nc.scalar.activation(out=r[:], in_=sum_sq[:], func=ACT.Abs_reciprocal_sqrt, scale=1.0 / HEAD_DIM, bias=EPS)
-            return (n, duo, xs, r)
-
-        def rotate(n, duo, xs, r):
-            e0, factors, out_rows = chunks[n][1], chunks[n][3], chunks[n][4]
-            for i in range(DUO):
-                t = DUO * duo + i
-                terms = terms_pool.tile([P, CHUNK_HEADS, 2, PAIRS, 2], F32, name="terms")
-                for h in range(CHUNK_HEADS):
-                    k = i * CHUNK_HEADS + h
-                    nc.vector.scalar_tensor_tensor(
-                        out=terms[:, h].rearrange("p o i j -> p o (i j)"),
-                        in0=xs[i][:, h * HEAD_DIM : (h + 1) * HEAD_DIM].unsqueeze(1).to_broadcast([P, 2, HEAD_DIM]),
-                        scalar=r[:, k : k + 1],
-                        in1=factors[:, t],
-                        op0=ALU.mult,
-                        op1=ALU.mult,
-                    )
-                rotated = rotated_pool.tile([P, CHUNK_HEADS, PAIRS, 2], F32, name="rotated")
-                by_output = terms[:].rearrange("p h o i j -> p h i o j")
-                nc.gpsimd.tensor_tensor(
-                    out=rotated[:], in0=by_output[:, :, :, :, 0], in1=by_output[:, :, :, :, 1], op=ALU.add
+            acc = psum_acc.tile([P, CHUNK], F32, name="acc")
+            for g in range(PASSES):
+                nc.tensor.matmul_mx(
+                    out=acc[:],
+                    lhsT=x_codes[:, g, t * P : (t + 1) * P].bitcast(FP8X4),
+                    lhsT_scale=x_scales[:, g, t * P : (t + 1) * P],
+                    rhs=w_codes[n][:, g, :].bitcast(FP8X4),
+                    rhs_scale=w_scales[n][:, g, :],
+                    start=(g == 0),
+                    stop=(g == PASSES - 1),
                 )
-                nc.sync.dma_start(out=out_rows[:, t, e0 : e0 + CHUNK], in_=rotated[:].rearrange("p h i o -> p (h i o)"))
+            x = acc
+            if bias_col is not None:
+                x = work.tile([P, CHUNK], F32, name="biased")
+                nc.vector.tensor_tensor(out=x[:], in0=acc[:], in1=bias_sb[:, bias_col : bias_col + CHUNK], op=ALU.add)
+
+            squares = work.tile([P, CHUNK], BF16, name="squares")
+            sum_sq = small.tile([P, CHUNK_HEADS], F32, name="sum_sq")
+            for h in range(CHUNK_HEADS):
+                head = slice(h * HEAD_DIM, (h + 1) * HEAD_DIM)
+                nc.scalar.activation(
+                    out=squares[:, head], in_=x[:, head], func=ACT.Square, accum_out=sum_sq[:, h : h + 1]
+                )
+            r = small.tile([P, CHUNK_HEADS], F32, name="r")
+            nc.scalar.activation(out=r[:], in_=sum_sq[:], func=ACT.Abs_reciprocal_sqrt, scale=1.0 / HEAD_DIM, bias=EPS)
+            return (n, t, x, r)
+
+        def rotate(n, t, x, r):
+            e0, factors, out_rows = chunks[n][1], chunks[n][3], chunks[n][4]
+            terms = terms_pool.tile([P, CHUNK_HEADS, 2, PAIRS, 2], F32, name="terms")
+            for h in range(CHUNK_HEADS):
+                nc.vector.scalar_tensor_tensor(
+                    out=terms[:, h].rearrange("p o i j -> p o (i j)"),
+                    in0=x[:, h * HEAD_DIM : (h + 1) * HEAD_DIM].unsqueeze(1).to_broadcast([P, 2, HEAD_DIM]),
+                    scalar=r[:, h : h + 1],
+                    in1=factors[:, t],
+                    op0=ALU.mult,
+                    op1=ALU.mult,
+                )
+            rotated = rotated_pool.tile([P, CHUNK_HEADS, PAIRS, 2], F32, name="rotated")
+            by_output = terms[:].rearrange("p h o i j -> p h i o j")
+            nc.gpsimd.tensor_tensor(out=rotated[:], in0=by_output[:, :, :, :, 0], in1=by_output[:, :, :, :, 1], op=ALU.add)
+            nc.sync.dma_start(out=out_rows[:, t, e0 : e0 + CHUNK], in_=rotated[:].rearrange("p h i o -> p (h i o)"))
 
         nc.vector.tensor_copy(out=rot[:, :, 0, :, 0], in_=cos_sb[:, :, :, 0])
         nc.vector.tensor_scalar_mul(out=rot[:, :, 0, :, 1], in0=sin_sb[:, :, :, 0], scalar1=-1.0)
@@ -265,34 +254,29 @@ def tile_flux2attention_pa_kernel(
                 op=ALU.mult,
             )
 
-        for g in range(PASSES):
-            quantise(*transpose_x(first_duos[0], g, vector_helps=True))
+        for i, unit in enumerate(units[0:PASSES]):
+            quantise(*transpose_unit(*unit, vector_copies=(i % 2 == 1)))
         spread(gain_rows[:], gain_sb[:].rearrange("p i d -> p (i d)"))
-        for n, g in units[0:PASSES]:
-            quantise(*transpose_w(n, g, vector_helps=True))
+        for i, unit in enumerate(units[PASSES:units_before_the_loop]):
+            quantise(*transpose_unit(*unit, vector_copies=(i % 2 == 1)))
         for i, factors in enumerate((factors_q, factors_k)):
             build_factors(factors, TEXT_TILES, TILES - TEXT_TILES, i)
             build_factors(factors, 0, TEXT_TILES, 2 + i)
         spread_bias(1)
 
-        prepared = PASSES
+        prepared = units_before_the_loop
         multiplied = None
-        for step, (n, duo) in enumerate(works):
+        for step, (n, t) in enumerate(works):
             if step == 0 or works[step - 1][0] != n:
                 if n + RAW_CHUNKS < len(chunks):
                     load_chunk(n + RAW_CHUNKS)
                 if chunks[n][2] is not None and n + 2 < len(chunks):
                     spread_bias(n + 2)
-            copied = []
-            if step + 1 < len(first_duos):
-                for g in range(PASSES):
-                    copied.append(transpose_x(first_duos[step + 1], g))
-            wanted = min(len(units), PASSES * step, 3 * (step + 1 + LEAD) // 2)
-            for n_ahead, g in units[prepared:wanted]:
-                copied.append(transpose_w(n_ahead, g))
+            wanted = units_before_the_loop + min(UNITS_A_STEP_AT_FIRST * (step + 1), 3 * (step + 1 + LEAD) // 2)
+            copied = [transpose_unit(*unit) for unit in units[prepared:wanted]]
             prepared = max(prepared, wanted)
             before = multiplied
-            multiplied = project(n, duo)
+            multiplied = project(n, t)
             if before is not None:
                 rotate(*before)
             for piece in copied:

@@ -88,8 +88,8 @@ def tile_flux2attention_pa_kernel(
         ones = const.tile([P, P], BF16)
         ident = const.tile([P, P], F32)
         rot = const.tile([P, TILES, 2, PAIRS, 2], F32)
-        factors_q = const.tile([P, TILES, 2, HEAD_DIM], F32)
-        factors_k = const.tile([P, TILES, 2, HEAD_DIM], F32)
+        factors_q = const.tile([P, TILES, HEAD_DIM, 2], F32)
+        factors_k = const.tile([P, TILES, HEAD_DIM, 2], F32)
 
         chunks = []
         for w_img, w_txt, bias_col, factors, out_rows in (
@@ -225,19 +225,18 @@ def tile_flux2attention_pa_kernel(
 
         def rotate(n, t, x, r):
             e0, factors, out_rows = chunks[n][1], chunks[n][3], chunks[n][4]
-            terms = terms_pool.tile([P, CHUNK_HEADS, 2, PAIRS, 2], F32, name="terms")
+            terms = terms_pool.tile([P, CHUNK_HEADS, PAIRS, 2, 2], F32, name="terms")
             for h in range(CHUNK_HEADS):
                 nc.vector.scalar_tensor_tensor(
-                    out=terms[:, h].rearrange("p o i j -> p o (i j)"),
-                    in0=x[:, h * HEAD_DIM : (h + 1) * HEAD_DIM].unsqueeze(1).to_broadcast([P, 2, HEAD_DIM]),
+                    out=terms[:, h].rearrange("p i j o -> p (i j) o"),
+                    in0=x[:, h * HEAD_DIM : (h + 1) * HEAD_DIM].unsqueeze(2).to_broadcast([P, HEAD_DIM, 2]),
                     scalar=r[:, h : h + 1],
                     in1=factors[:, t],
                     op0=ALU.mult,
                     op1=ALU.mult,
                 )
             rotated = rotated_pool.tile([P, CHUNK_HEADS, PAIRS, 2], F32, name="rotated")
-            by_output = terms[:].rearrange("p h o i j -> p h i o j")
-            nc.gpsimd.tensor_tensor(out=rotated[:], in0=by_output[:, :, :, :, 0], in1=by_output[:, :, :, :, 1], op=ALU.add)
+            nc.gpsimd.tensor_tensor(out=rotated[:], in0=terms[:, :, :, 0, :], in1=terms[:, :, :, 1, :], op=ALU.add)
             nc.sync.dma_start(out=out_rows[:, t, e0 : e0 + CHUNK], in_=rotated[:].rearrange("p h i o -> p (h i o)"))
 
         nc.vector.tensor_copy(out=rot[:, :, 0, :, 0], in_=cos_sb[:, :, :, 0])
@@ -248,9 +247,9 @@ def tile_flux2attention_pa_kernel(
         def build_factors(factors, first_tile, n_tiles, gain_index):
             tiles = slice(first_tile, first_tile + n_tiles)
             nc.vector.tensor_tensor(
-                out=factors[:, tiles].rearrange("p t o d -> p (t o) d"),
-                in0=rot[:, tiles].rearrange("p t o i j -> p (t o) (i j)"),
-                in1=gain_sb[:, gain_index : gain_index + 1, :].to_broadcast([P, n_tiles * 2, HEAD_DIM]),
+                out=factors[:, tiles],
+                in0=rot[:, tiles].rearrange("p t o i j -> p t (i j) o"),
+                in1=gain_sb[:, gain_index : gain_index + 1, :].unsqueeze(3).to_broadcast([P, n_tiles, HEAD_DIM, 2]),
                 op=ALU.mult,
             )
 

@@ -66,8 +66,9 @@ def tile_flux2attention_pa_kernel(
         terms_pool = ctx.enter_context(tc.tile_pool(name="terms", bufs=5))
         rotated_pool = ctx.enter_context(tc.tile_pool(name="rotated", bufs=6))
         small = ctx.enter_context(tc.tile_pool(name="small", bufs=6))
-        psum_t = ctx.enter_context(tc.psum_pool(name="psum_t", bufs=4))
+        psum_t = ctx.enter_context(tc.psum_pool(name="psum_t", bufs=3))
         psum_acc = ctx.enter_context(tc.psum_pool(name="psum_acc", bufs=4))
+        psum_table = ctx.enter_context(tc.psum_pool(name="psum_table", bufs=1))
 
         x_txt = encoder_hidden_states[0].rearrange("(t p) k -> p t k", p=P)
         x_img = hidden_states[0].rearrange("(t p) k -> p t k", p=P)
@@ -223,8 +224,24 @@ def tile_flux2attention_pa_kernel(
             nc.scalar.activation(out=r[:], in_=sum_sq[:], func=ACT.Abs_reciprocal_sqrt, scale=1.0 / HEAD_DIM, bias=EPS)
             return (n, t, x, r)
 
+        text_factors = {}
+
+        def park_text_factors(factors):
+            table = factors[:, 0:TEXT_TILES].rearrange("p t d o -> p (t d o)")
+            flipped_bank = psum_t.tile([P, CHUNK], F32, name="xt")
+            for b in range(CHUNK // P):
+                nc.tensor.transpose(flipped_bank[:, b * P : (b + 1) * P], table[:, b * P : (b + 1) * P], ident[:])
+            flipped = work.tile([P, CHUNK], F32, name="flipped")
+            nc.scalar.copy(out=flipped[:], in_=flipped_bank[:])
+            text_factors[0] = psum_table.tile([P, TEXT_TILES, HEAD_DIM, 2], F32, name="text_factors")
+            parked = text_factors[0][:].rearrange("p t d o -> p (t d o)")
+            for b in range(CHUNK // P):
+                nc.tensor.transpose(parked[:, b * P : (b + 1) * P], flipped[:, b * P : (b + 1) * P], ident[:])
+
         def rotate(n, t, x, r):
             e0, factors, out_rows = chunks[n][1], chunks[n][3], chunks[n][4]
+            if t < TEXT_TILES:
+                factors = text_factors[0]
             terms = terms_pool.tile([P, CHUNK_HEADS, PAIRS, 2, 2], F32, name="terms")
             for h in range(CHUNK_HEADS):
                 nc.vector.scalar_tensor_tensor(
@@ -271,6 +288,8 @@ def tile_flux2attention_pa_kernel(
                     load_chunk(n + RAW_CHUNKS)
                 if chunks[n][2] is not None and n + 2 < len(chunks):
                     spread_bias(n + 2)
+                if chunks[n][2] is not None and chunks[n][1] == 0:
+                    park_text_factors(chunks[n][3])
             wanted = units_before_the_loop + min(UNITS_A_STEP_AT_FIRST * (step + 1), 3 * (step + 1 + LEAD) // 2)
             copied = [transpose_unit(*unit) for unit in units[prepared:wanted]]
             prepared = max(prepared, wanted)

from contextlib import ExitStack

import concourse.mybir as mybir
from concourse.masks import make_identity

F32 = mybir.dt.float32
BF16 = mybir.dt.bfloat16
I32 = mybir.dt.int32
U32 = mybir.dt.uint32
U8 = mybir.dt.uint8
FP8X4 = mybir.dt.float8_e4m3fn_x4
ACT = mybir.ActivationFunctionType
ALU = mybir.AluOpType

P = 128
D_MODEL = 1536
WORDS = D_MODEL // 2
K_PASS = 512
PASSES = D_MODEL // K_PASS
HEAD_DIM = 128
PAIRS = HEAD_DIM // 2
E_OUT = 1536
CHUNK = 512
CHUNK_HEADS = CHUNK // HEAD_DIM
CHUNK_ROW_TILES = CHUNK // P
CHUNKS = E_OUT // CHUNK
TILES = 8
TEXT_TILES = 2
UNIT_ROW_TILES = 2
UNIT_ROWS = UNIT_ROW_TILES * P
EPS = 1e-5
RAW_CHUNKS = 4
UNITS_A_STEP_AT_FIRST = 3
LEAD = 7

FLOPS = 2 * 2 * 1024 * D_MODEL * E_OUT


def tile_flux2attention_pa_kernel(
    tc,
    hidden_states,
    encoder_hidden_states,
    rope_cos,
    rope_sin,
    Wq,
    Wk,
    Waq,
    baq,
    Wak,
    bak,
    wq_norm,
    wk_norm,
    waq_norm,
    wak_norm,
    out_0,
    out_1,
):
    nc = tc.nc
    with ExitStack() as ctx:
        ctx.enter_context(tc.manual_schedule())
        const = ctx.enter_context(tc.tile_pool(name="const", bufs=1))
        raw_pool = ctx.enter_context(tc.tile_pool(name="raw", bufs=RAW_CHUNKS))
        grouped_pool = ctx.enter_context(tc.tile_pool(name="grouped", bufs=8))
        quant_pool = ctx.enter_context(tc.tile_pool(name="quant", bufs=3))
        work = ctx.enter_context(tc.tile_pool(name="work", bufs=3))
        terms_pool = ctx.enter_context(tc.tile_pool(name="terms", bufs=5))
        rotated_pool = ctx.enter_context(tc.tile_pool(name="rotated", bufs=6))
        small = ctx.enter_context(tc.tile_pool(name="small", bufs=6))
        psum_t = ctx.enter_context(tc.psum_pool(name="psum_t", bufs=3))
        psum_acc = ctx.enter_context(tc.psum_pool(name="psum_acc", bufs=4))
        psum_table = ctx.enter_context(tc.psum_pool(name="psum_table", bufs=1))

        x_txt = encoder_hidden_states[0].rearrange("(t p) k -> p t k", p=P)
        x_img = hidden_states[0].rearrange("(t p) k -> p t k", p=P)
        out_q = out_0[0].rearrange("(t p) h d -> p t (h d)", p=P)
        out_k = out_1[0].rearrange("(t p) h d -> p t (h d)", p=P)

        x_raw = const.tile([P, TILES, D_MODEL], BF16)
        x_codes = const.tile([P, PASSES, TILES * P], U32, align_bytes=64)
        x_scales = const.tile([P, PASSES, TILES * P], U8, align_bytes=64)
        cos_sb = const.tile([P, TILES, PAIRS, 2], BF16)
        sin_sb = const.tile([P, TILES, PAIRS, 2], BF16)
        gain_rows = const.tile([P, 4 * HEAD_DIM], BF16)
        bias_rows = const.tile([P, 2 * E_OUT], BF16)
        gain_sb = const.tile([P, 4, HEAD_DIM], BF16)
        bias_sb = const.tile([P, 2 * E_OUT], BF16)
        one = const.tile([P, 1], F32)
        unused = const.tile([P, 1], F32)
        ones = const.tile([P, P], BF16)
        ident = const.tile([P, P], F32)
        rot = const.tile([P, TILES, 2, PAIRS, 2], F32)
        factors_q = const.tile([P, TILES, HEAD_DIM, 2], F32)
        factors_k = const.tile([P, TILES, HEAD_DIM, 2], F32)

        chunks = []
        for w_img, w_txt, bias_col, factors, out_rows in (
            (Wq, Waq, 0, factors_q, out_q),
            (Wk, Wak, E_OUT, factors_k, out_k),
        ):
            for c in range(CHUNKS):
                chunks.append((w_img, c * CHUNK, None, factors, out_rows, range(TEXT_TILES, TILES)))
                chunks.append((w_txt, c * CHUNK, bias_col + c * CHUNK, factors, out_rows, range(TEXT_TILES)))
        works = [(n, t) for n in range(len(chunks)) for t in chunks[n][5]]

        needs = []
        for n, t in works:
            for need in (("x", t // UNIT_ROW_TILES), ("w", n)):
                if need not in needs:
                    needs.append(need)
        units = []
        for kind, which in needs:
            row_tiles = UNIT_ROW_TILES if kind == "x" else CHUNK_ROW_TILES
            for g in range(PASSES):
                for r in range(0, row_tiles, UNIT_ROW_TILES):
                    units.append((kind, which, g, r))
        units_before_the_loop = PASSES + PASSES * CHUNK_ROW_TILES // UNIT_ROW_TILES

        def load_tokens(pair):
            t0 = UNIT_ROW_TILES * pair
            stream, first = (x_txt, t0) if t0 < TEXT_TILES else (x_img, t0 - TEXT_TILES)
            nc.sync.dma_start(out=x_raw[:, t0 : t0 + UNIT_ROW_TILES, :], in_=stream[:, first : first + UNIT_ROW_TILES, :])

        w_raw = {}

        def load_chunk(n, pieces=1):
            weight, e0 = chunks[n][0], chunks[n][1]
            w_raw[n] = raw_pool.tile([P, CHUNK_ROW_TILES, D_MODEL], BF16, name="w_raw")
            rows = weight[e0 : e0 + CHUNK, :].rearrange("(r p) k -> p r k", p=P)
            for i in range(pieces):
                k_range = slice(i * D_MODEL // pieces, (i + 1) * D_MODEL // pieces)
                nc.sync.dma_start(out=w_raw[n][:, :, k_range], in_=rows[:, :, k_range])

        nc.vector.memset(gain_rows[:].bitcast(I32), 0)
        nc.vector.memset(bias_rows[:].bitcast(I32), 0)
        nc.vector.memset(ones[:], 1.0)
        nc.vector.memset(one[:], 1.0)
        make_identity(nc, ident[:])

        for i, gain in enumerate((wq_norm, wk_norm, waq_norm, wak_norm)):
            nc.scalar.dma_start(
                out=gain_rows[0:1, i * HEAD_DIM : (i + 1) * HEAD_DIM], in_=gain.rearrange("(o d) -> o d", o=1)
            )
        for table_sb, table in ((cos_sb, rope_cos), (sin_sb, rope_sin)):
            nc.scalar.dma_start(
                out=table_sb[:].rearrange("p t i j -> p t (i j)"), in_=table.rearrange("(t p) d -> p t d", p=P)
            )
        nc.scalar.activation(out=unused[:], in_=one[:], func=ACT.Abs_reciprocal_sqrt)
        for i, bias in enumerate((baq, bak)):
            nc.gpsimd.dma_start(
                out=bias_rows[0:1, i * E_OUT : (i + 1) * E_OUT], in_=bias.rearrange("(o e) -> o e", o=1)
            )
        for kind, which in needs:
            if kind == "x":
                load_tokens(which)
            elif which < RAW_CHUNKS:
                load_chunk(which, pieces=(PASSES if which == 0 else 1))

        def spread(rows, target):
            bank = psum_acc.tile([P, CHUNK], F32, name="acc")
            nc.tensor.matmul(out=bank[:], lhsT=ones[:], rhs=rows, start=True, stop=True)
            nc.scalar.copy(out=target, in_=bank[:])

        def spread_bias(n):
            cols = slice(chunks[n][2], chunks[n][2] + CHUNK)
            spread(bias_rows[:, cols], bias_sb[:, cols])

        w_codes = {}
        w_scales = {}

        def transpose_unit(kind, which, g, r0, vector_copies=False):
            if kind == "x":
                words = x_raw[:].rearrange("p t k -> p (t k)").bitcast(F32)
                r0 = UNIT_ROW_TILES * which
                codes, scales = x_codes, x_scales
            else:
                if g == 0 and r0 == 0:
                    w_codes[which] = quant_pool.tile([P, PASSES, CHUNK], U32, align_bytes=64, name="w_codes")
                    w_scales[which] = quant_pool.tile([P, PASSES, CHUNK], U8, align_bytes=64, name="w_scales")
                words = w_raw[which][:].rearrange("p r k -> p (r k)").bitcast(F32)
                codes, scales = w_codes[which], w_scales[which]
            xt = psum_t.tile([P, 2, UNIT_ROWS], F32, name="xt")
            for u in range(2):
                for r in range(UNIT_ROW_TILES):
                    word = (r0 + r) * WORDS + (K_PASS // 2) * g + P * u
                    nc.tensor.transpose(xt[:, u, r * P : (r + 1) * P], words[:, word : word + P], ident[:])
            grouped = grouped_pool.tile([P, 4 * UNIT_ROWS], BF16, align_bytes=64, name="grouped")
            grouped_words = grouped[:].bitcast(F32).rearrange("p (c u) -> p c u", u=2)
            if vector_copies:
                nc.vector.tensor_copy(out=grouped_words, in_=xt[:].rearrange("p u c -> p c u"))
            else:
                nc.scalar.copy(out=grouped_words, in_=xt[:].rearrange("p u c -> p c u"))
            cols = slice(r0 * P, r0 * P + UNIT_ROWS)
            return (grouped[:], codes[:, g, cols], scales[:, g, cols])

        def quantise(grouped, codes, scales):
            nc.vector.quantize_mx(out=codes.bitcast(FP8X4), scales=scales, in_=grouped)

        def project(n, t):
            bias_col = chunks[n][2]
            acc = psum_acc.tile([P, CHUNK], F32, name="acc")
            for g in range(PASSES):
                nc.tensor.matmul_mx(
                    out=acc[:],
                    lhsT=x_codes[:, g, t * P : (t + 1) * P].bitcast(FP8X4),
                    lhsT_scale=x_scales[:, g, t * P : (t + 1) * P],
                    rhs=w_codes[n][:, g, :].bitcast(FP8X4),
                    rhs_scale=w_scales[n][:, g, :],
                    start=(g == 0),
                    stop=(g == PASSES - 1),
                )
            x = acc
            if bias_col is not None:
                x = work.tile([P, CHUNK], F32, name="biased")
                nc.vector.tensor_tensor(out=x[:], in0=acc[:], in1=bias_sb[:, bias_col : bias_col + CHUNK], op=ALU.add)

            squares = work.tile([P, CHUNK], BF16, name="squares")
            sum_sq = small.tile([P, CHUNK_HEADS], F32, name="sum_sq")
            for h in range(CHUNK_HEADS):
                head = slice(h * HEAD_DIM, (h + 1) * HEAD_DIM)
                nc.scalar.activation(
                    out=squares[:, head], in_=x[:, head], func=ACT.Square, accum_out=sum_sq[:, h : h + 1]
                )
            r = small.tile([P, CHUNK_HEADS], F32, name="r")
            nc.scalar.activation(out=r[:], in_=sum_sq[:], func=ACT.Abs_reciprocal_sqrt, scale=1.0 / HEAD_DIM, bias=EPS)
            return (n, t, x, r)

        text_factors = {}

        def park_text_factors(factors):
            table = factors[:, 0:TEXT_TILES].rearrange("p t d o -> p (t d o)")
            flipped_bank = psum_t.tile([P, CHUNK], F32, name="xt")
            for b in range(CHUNK // P):
                nc.tensor.transpose(flipped_bank[:, b * P : (b + 1) * P], table[:, b * P : (b + 1) * P], ident[:])
            flipped = work.tile([P, CHUNK], F32, name="flipped")
            nc.scalar.copy(out=flipped[:], in_=flipped_bank[:])
            text_factors[0] = psum_table.tile([P, TEXT_TILES, HEAD_DIM, 2], F32, name="text_factors")
            parked = text_factors[0][:].rearrange("p t d o -> p (t d o)")
            for b in range(CHUNK // P):
                nc.tensor.transpose(parked[:, b * P : (b + 1) * P], flipped[:, b * P : (b + 1) * P], ident[:])

        def rotate(n, t, x, r):
            e0, factors, out_rows = chunks[n][1], chunks[n][3], chunks[n][4]
            if t < TEXT_TILES:
                factors = text_factors[0]
            terms = terms_pool.tile([P, CHUNK_HEADS, PAIRS, 2, 2], F32, name="terms")
            for h in range(CHUNK_HEADS):
                nc.vector.scalar_tensor_tensor(
                    out=terms[:, h].rearrange("p i j o -> p (i j) o"),
                    in0=x[:, h * HEAD_DIM : (h + 1) * HEAD_DIM].unsqueeze(2).to_broadcast([P, HEAD_DIM, 2]),
                    scalar=r[:, h : h + 1],
                    in1=factors[:, t],
                    op0=ALU.mult,
                    op1=ALU.mult,
                )
            rotated = rotated_pool.tile([P, CHUNK_HEADS, PAIRS, 2], F32, name="rotated")
            nc.gpsimd.tensor_tensor(out=rotated[:], in0=terms[:, :, :, 0, :], in1=terms[:, :, :, 1, :], op=ALU.add)
            nc.sync.dma_start(out=out_rows[:, t, e0 : e0 + CHUNK], in_=rotated[:].rearrange("p h i o -> p (h i o)"))

        nc.vector.tensor_copy(out=rot[:, :, 0, :, 0], in_=cos_sb[:, :, :, 0])
        nc.vector.tensor_scalar_mul(out=rot[:, :, 0, :, 1], in0=sin_sb[:, :, :, 0], scalar1=-1.0)
        nc.vector.tensor_copy(out=rot[:, :, 1, :, 0], in_=sin_sb[:, :, :, 1])
        nc.vector.tensor_copy(out=rot[:, :, 1, :, 1], in_=cos_sb[:, :, :, 1])

        def build_factors(factors, first_tile, n_tiles, gain_index):
            tiles = slice(first_tile, first_tile + n_tiles)
            nc.vector.tensor_tensor(
                out=factors[:, tiles],
                in0=rot[:, tiles].rearrange("p t o i j -> p t (i j) o"),
                in1=gain_sb[:, gain_index : gain_index + 1, :].unsqueeze(3).to_broadcast([P, n_tiles, HEAD_DIM, 2]),
                op=ALU.mult,
            )

        for i, unit in enumerate(units[0:PASSES]):
            quantise(*transpose_unit(*unit, vector_copies=(i % 2 == 1)))
        spread(gain_rows[:], gain_sb[:].rearrange("p i d -> p (i d)"))
        for i, unit in enumerate(units[PASSES:units_before_the_loop]):
            quantise(*transpose_unit(*unit, vector_copies=(i % 2 == 1)))
        for i, factors in enumerate((factors_q, factors_k)):
            build_factors(factors, TEXT_TILES, TILES - TEXT_TILES, i)
            build_factors(factors, 0, TEXT_TILES, 2 + i)
        spread_bias(1)

        prepared = units_before_the_loop
        multiplied = None
        for step, (n, t) in enumerate(works):
            if step == 0 or works[step - 1][0] != n:
                if n + RAW_CHUNKS < len(chunks):
                    load_chunk(n + RAW_CHUNKS)
                if chunks[n][2] is not None and n + 2 < len(chunks):
                    spread_bias(n + 2)
                if chunks[n][2] is not None and chunks[n][1] == 0:
                    park_text_factors(chunks[n][3])
            wanted = units_before_the_loop + min(UNITS_A_STEP_AT_FIRST * (step + 1), 3 * (step + 1 + LEAD) // 2)
            copied = [transpose_unit(*unit) for unit in units[prepared:wanted]]
            prepared = max(prepared, wanted)
            before = multiplied
            multiplied = project(n, t)
            if before is not None:
                rotate(*before)
            for piece in copied:
                quantise(*piece)
        rotate(*multiplied)
